import numpy as np
import ml_dtypes

BF16 = ml_dtypes.bfloat16


def bf(x):
    return np.asarray(x, np.float32).astype(BF16)


def f32(x):
    return np.asarray(x, np.float32)


def f64(x):
    return np.asarray(x).astype(np.float64)


def striped(idx):
    return np.tile(idx.reshape(-1, 16).T, (8, 1))


C, S, N, H = 128, 1024, 1024, 384


def sigmoid(a):
    return 1.0 / (1.0 + np.exp(-a))


def setup_inputs():
    return {"x": bf(np.random.standard_normal((C, S))), "w": bf(np.random.standard_normal((C, C)) / np.sqrt(C)), "w_ih": bf(np.random.standard_normal((C, H)) / np.sqrt(C)), "w_hh": bf(np.random.standard_normal((C, H)) / np.sqrt(C)), "b_ih": f32(0.2 * np.random.standard_normal((H, 1))), "b_hh": f32(0.2 * np.random.standard_normal((H, 1))), "offs": striped(np.random.permutation(np.tile(np.arange(S), 2))[:N])}


def reference(x, w, w_ih, w_hh, b_ih, b_hh, offs):
    idx = offs[:16].T.reshape(-1)
    h = f64(x)
    m = f64(w).T @ h[:, idx]
    u = f64(w_ih).T @ m + f64(b_ih)
    v = f64(w_hh).T @ h + f64(b_hh)
    r = sigmoid(u[:C] + v[:C])
    z = sigmoid(u[C:H - C] + v[C:H - C])
    cand = np.tanh(u[H - C:] + r * v[H - C:])
    return (1.0 - z) * cand + z * h

@@ -1,0 +1,86 @@
+import concourse.mybir as mybir
+
+BF16, F32, U16 = mybir.dt.bfloat16, mybir.dt.float32, mybir.dt.uint16
+ADD, SUBTRACT, MULT = mybir.AluOpType.add, mybir.AluOpType.subtract, mybir.AluOpType.mult
+SIGMOID, TANH = mybir.ActivationFunctionType.Sigmoid, mybir.ActivationFunctionType.Tanh
+
+C = 128
+S = 1024
+N = 1024
+PIECE = 512
+PIECES = N // PIECE
+LIST_COLS = PIECE // 16
+
+FLOPS = 2 * C * C * N + 2 * 2 * C * 3 * C * N
+
+
+def tile_denseggnn_kernel(tc, x, w, w_ih, w_hh, b_ih, b_hh, offs, out):
+    nc = tc.nc
+    with (
+        tc.tile_pool(name="held", bufs=1) as held,
+        tc.tile_pool(name="work", bufs=2) as work,
+        tc.psum_pool(name="gates", bufs=2) as gates,
+        tc.psum_pool(name="turns", bufs=4) as turns,
+    ):
+        offsets = held.tile([C, N // 16], U16, name="offsets")
+        nc.sync.dma_start(offsets[:], offs)
+        x_sb = held.tile([C, S], BF16, name="x_sb")
+        nc.sync.dma_start(x_sb[:], x)
+        w_sb = held.tile([C, C], BF16, name="w_sb")
+        nc.scalar.dma_start(w_sb[:], w)
+        w_hh_sb = held.tile([C, 3 * C], BF16, name="w_hh_sb")
+        nc.scalar.dma_start(w_hh_sb[:], w_hh)
+        w_ih_sb = held.tile([C, 3 * C], BF16, name="w_ih_sb")
+        nc.scalar.dma_start(w_ih_sb[:], w_ih)
+
+        bias_ih = held.tile([C, 3], F32, name="bias_ih")
+        bias_hh = held.tile([C, 3], F32, name="bias_hh")
+        with nc.allow_non_contiguous_dma(reason="one bias value for each partition"):
+            nc.gpsimd.dma_start(bias_ih[:], b_ih.rearrange("(g c) o -> c (g o)", c=C))
+            nc.gpsimd.dma_start(bias_hh[:], b_hh.rearrange("(g c) o -> c (g o)", c=C))
+        bias_rz = held.tile([C, 2], F32, name="bias_rz")
+        nc.vector.tensor_add(bias_rz[:], bias_ih[:, 0:2], bias_hh[:, 0:2])
+
+        messages = []
+        for p in range(PIECES):
+            m_ps = turns.tile([C, PIECE], F32, name=f"m_ps{p}", tag="turn")
+            picked = x_sb[:].indirect(offsets[:, p * LIST_COLS : (p + 1) * LIST_COLS])
+            nc.tensor.matmul(m_ps[:], w_sb[:], picked, start=True, stop=True)
+            m_bf = held.tile([C, PIECE], BF16, name=f"m_bf{p}")
+            nc.vector.tensor_copy(m_bf[:], m_ps[:])
+            messages.append(m_bf)
+
+        for p in range(PIECES):
+            own = x_sb[:, p * PIECE : (p + 1) * PIECE]
+            m_bf = messages[p]
+
+            r_ps = gates.tile([C, PIECE], F32, name="r_ps")
+            nc.tensor.matmul(r_ps[:], w_hh_sb[:, 0:C], own, start=True, stop=False)
+            nc.tensor.matmul(r_ps[:], w_ih_sb[:, 0:C], m_bf[:], start=False, stop=True)
+            vn_ps = turns.tile([C, PIECE], F32, name=f"vn_ps{p}", tag="turn")
+            nc.tensor.matmul(vn_ps[:], w_hh_sb[:, 2 * C : 3 * C], own, start=True, stop=True)
+            un_ps = turns.tile([C, PIECE], F32, name=f"un_ps{p}", tag="turn")
+            nc.tensor.matmul(un_ps[:], w_ih_sb[:, 2 * C : 3 * C], m_bf[:], start=True, stop=True)
+            z_ps = gates.tile([C, PIECE], F32, name="z_ps")
+            nc.tensor.matmul(z_ps[:], w_hh_sb[:, C : 2 * C], own, start=True, stop=False)
+            nc.tensor.matmul(z_ps[:], w_ih_sb[:, C : 2 * C], m_bf[:], start=False, stop=True)
+
+            r = work.tile([C, PIECE], F32, name="r")
+            nc.scalar.activation(r[:], r_ps[:], SIGMOID, bias=bias_rz[:, 0:1])
+            z = work.tile([C, PIECE], F32, name="z")
+            nc.scalar.activation(z[:], z_ps[:], SIGMOID, bias=bias_rz[:, 1:2])
+
+            gated = work.tile([C, PIECE], F32, name="gated")
+            nc.vector.scalar_tensor_tensor(gated[:], vn_ps[:], bias_hh[:, 2:3], r[:], ADD, MULT)
+            pre = work.tile([C, PIECE], F32, name="pre")
+            nc.vector.tensor_tensor(pre[:], un_ps[:], gated[:], ADD)
+            cand = work.tile([C, PIECE], F32, name="cand")
+            nc.scalar.activation(cand[:], pre[:], TANH, bias=bias_ih[:, 2:3])
+
+            diff = work.tile([C, PIECE], F32, name="diff")
+            nc.vector.tensor_tensor(diff[:], own, cand[:], SUBTRACT)
+            step = work.tile([C, PIECE], F32, name="step")
+            nc.vector.tensor_tensor(step[:], z[:], diff[:], MULT)
+            new = work.tile([C, PIECE], F32, name="new")
+            nc.vector.tensor_tensor(new[:], step[:], cand[:], ADD)
+            nc.sync.dma_start(out[:, p * PIECE : (p + 1) * PIECE], new[:])

@@ -3,6 +3,7 @@ import concourse.mybir as mybir
 BF16, F32, U16 = mybir.dt.bfloat16, mybir.dt.float32, mybir.dt.uint16
 ADD, SUBTRACT, MULT = mybir.AluOpType.add, mybir.AluOpType.subtract, mybir.AluOpType.mult
 SIGMOID, TANH = mybir.ActivationFunctionType.Sigmoid, mybir.ActivationFunctionType.Tanh
+COPY = mybir.ActivationFunctionType.Copy
 
 C = 128
 S = 1024
@@ -10,6 +11,7 @@ N = 1024
 PIECE = 512
 PIECES = N // PIECE
 LIST_COLS = PIECE // 16
+WARM_MATMULS = 4
 
 FLOPS = 2 * C * C * N + 2 * 2 * C * 3 * C * N
 
@@ -18,69 +20,85 @@ def tile_denseggnn_kernel(tc, x, w, w_ih, w_hh, b_ih, b_hh, offs, out):
     nc = tc.nc
     with (
         tc.tile_pool(name="held", bufs=1) as held,
-        tc.tile_pool(name="work", bufs=2) as work,
-        tc.psum_pool(name="gates", bufs=2) as gates,
+        tc.tile_pool(name="work", bufs=PIECES) as work,
+        tc.psum_pool(name="gates", bufs=PIECES) as gates,
         tc.psum_pool(name="turns", bufs=4) as turns,
     ):
         offsets = held.tile([C, N // 16], U16, name="offsets")
         nc.sync.dma_start(offsets[:], offs)
         x_sb = held.tile([C, S], BF16, name="x_sb")
-        nc.sync.dma_start(x_sb[:], x)
+        nc.scalar.dma_start(x_sb[:], x)
         w_sb = held.tile([C, C], BF16, name="w_sb")
-        nc.scalar.dma_start(w_sb[:], w)
+        nc.sync.dma_start(w_sb[:], w)
         w_hh_sb = held.tile([C, 3 * C], BF16, name="w_hh_sb")
         nc.scalar.dma_start(w_hh_sb[:], w_hh)
         w_ih_sb = held.tile([C, 3 * C], BF16, name="w_ih_sb")
-        nc.scalar.dma_start(w_ih_sb[:], w_ih)
+        nc.sync.dma_start(w_ih_sb[:], w_ih)
 
         bias_ih = held.tile([C, 3], F32, name="bias_ih")
         bias_hh = held.tile([C, 3], F32, name="bias_hh")
         with nc.allow_non_contiguous_dma(reason="one bias value for each partition"):
-            nc.gpsimd.dma_start(bias_ih[:], b_ih.rearrange("(g c) o -> c (g o)", c=C))
-            nc.gpsimd.dma_start(bias_hh[:], b_hh.rearrange("(g c) o -> c (g o)", c=C))
+            nc.sync.dma_start(bias_ih[:], b_ih.rearrange("(g c) o -> c (g o)", c=C))
+            nc.sync.dma_start(bias_hh[:], b_hh.rearrange("(g c) o -> c (g o)", c=C))
         bias_rz = held.tile([C, 2], F32, name="bias_rz")
-        nc.vector.tensor_add(bias_rz[:], bias_ih[:, 0:2], bias_hh[:, 0:2])
+        nc.gpsimd.tensor_tensor(bias_rz[:], bias_ih[:, 0:2], bias_hh[:, 0:2], ADD)
 
-        messages = []
+        zeros = held.tile([C, PIECE], BF16, name="zeros")
+        nc.gpsimd.memset(zeros[:], 0.0)
+        idle_ps = turns.tile([C, PIECE], F32, name="idle_ps", tag="turn")
+        for i in range(WARM_MATMULS):
+            nc.tensor.matmul(idle_ps[:], zeros[:, 0:C], zeros[:], start=True, stop=True)
+        idle_act = held.tile([C, 1], F32, name="idle_act")
+        nc.scalar.activation(idle_act[:], zeros[:, 0:1], SIGMOID)
+
+        own = [x_sb[:, p * PIECE : (p + 1) * PIECE] for p in range(PIECES)]
+
+        m_bf = []
         for p in range(PIECES):
             m_ps = turns.tile([C, PIECE], F32, name=f"m_ps{p}", tag="turn")
             picked = x_sb[:].indirect(offsets[:, p * LIST_COLS : (p + 1) * LIST_COLS])
             nc.tensor.matmul(m_ps[:], w_sb[:], picked, start=True, stop=True)
-            m_bf = held.tile([C, PIECE], BF16, name=f"m_bf{p}")
-            nc.vector.tensor_copy(m_bf[:], m_ps[:])
-            messages.append(m_bf)
+            m_bf.append(held.tile([C, PIECE], BF16, name=f"m_bf{p}"))
+            if p % 2 == 0:
+                nc.vector.tensor_copy(m_bf[p][:], m_ps[:])
+            else:
+                nc.scalar.activation(m_bf[p][:], m_ps[:], COPY)
+
+        r_ps, vn_ps, un_ps, z_ps = [], [], [], []
+        for p in range(PIECES):
+            r_ps.append(gates.tile([C, PIECE], F32, name="r_ps"))
+            nc.tensor.matmul(r_ps[p][:], w_hh_sb[:, 0:C], own[p], start=True, stop=False)
+            nc.tensor.matmul(r_ps[p][:], w_ih_sb[:, 0:C], m_bf[p][:], start=False, stop=True)
+            vn_ps.append(turns.tile([C, PIECE], F32, name=f"vn_ps{p}", tag="turn"))
+            nc.tensor.matmul(vn_ps[p][:], w_hh_sb[:, 2 * C : 3 * C], own[p], start=True, stop=True)
+            un_ps.append(turns.tile([C, PIECE], F32, name=f"un_ps{p}", tag="turn"))
+            nc.tensor.matmul(un_ps[p][:], w_ih_sb[:, 2 * C : 3 * C], m_bf[p][:], start=True, stop=True)
+        for p in range(PIECES):
+            z_ps.append(gates.tile([C, PIECE], F32, name="z_ps"))
+            nc.tensor.matmul(z_ps[p][:], w_hh_sb[:, C : 2 * C], own[p], start=True, stop=False)
+            nc.tensor.matmul(z_ps[p][:], w_ih_sb[:, C : 2 * C], m_bf[p][:], start=False, stop=True)
+
+        r = []
+        for p in range(PIECES):
+            r.append(work.tile([C, PIECE], F32, name="r"))
+            nc.scalar.activation(r[p][:], r_ps[p][:], SIGMOID, bias=bias_rz[:, 0:1])
+
+        cand, z = [], []
+        for p in range(PIECES):
+            gated = work.tile([C, PIECE], F32, name="gated")
+            nc.vector.scalar_tensor_tensor(gated[:], vn_ps[p][:], bias_hh[:, 2:3], r[p][:], ADD, MULT)
+            pre = work.tile([C, PIECE], F32, name="pre")
+            nc.vector.tensor_tensor(pre[:], un_ps[p][:], gated[:], ADD)
+            cand.append(work.tile([C, PIECE], F32, name="cand"))
+            nc.scalar.activation(cand[p][:], pre[:], TANH, bias=bias_ih[:, 2:3])
+            z.append(work.tile([C, PIECE], F32, name="z"))
+            nc.scalar.activation(z[p][:], z_ps[p][:], SIGMOID, bias=bias_rz[:, 1:2])
 
         for p in range(PIECES):
-            own = x_sb[:, p * PIECE : (p + 1) * PIECE]
-            m_bf = messages[p]
-
-            r_ps = gates.tile([C, PIECE], F32, name="r_ps")
-            nc.tensor.matmul(r_ps[:], w_hh_sb[:, 0:C], own, start=True, stop=False)
-            nc.tensor.matmul(r_ps[:], w_ih_sb[:, 0:C], m_bf[:], start=False, stop=True)
-            vn_ps = turns.tile([C, PIECE], F32, name=f"vn_ps{p}", tag="turn")
-            nc.tensor.matmul(vn_ps[:], w_hh_sb[:, 2 * C : 3 * C], own, start=True, stop=True)
-            un_ps = turns.tile([C, PIECE], F32, name=f"un_ps{p}", tag="turn")
-            nc.tensor.matmul(un_ps[:], w_ih_sb[:, 2 * C : 3 * C], m_bf[:], start=True, stop=True)
-            z_ps = gates.tile([C, PIECE], F32, name="z_ps")
-            nc.tensor.matmul(z_ps[:], w_hh_sb[:, C : 2 * C], own, start=True, stop=False)
-            nc.tensor.matmul(z_ps[:], w_ih_sb[:, C : 2 * C], m_bf[:], start=False, stop=True)
-
-            r = work.tile([C, PIECE], F32, name="r")
-            nc.scalar.activation(r[:], r_ps[:], SIGMOID, bias=bias_rz[:, 0:1])
-            z = work.tile([C, PIECE], F32, name="z")
-            nc.scalar.activation(z[:], z_ps[:], SIGMOID, bias=bias_rz[:, 1:2])
-
-            gated = work.tile([C, PIECE], F32, name="gated")
-            nc.vector.scalar_tensor_tensor(gated[:], vn_ps[:], bias_hh[:, 2:3], r[:], ADD, MULT)
-            pre = work.tile([C, PIECE], F32, name="pre")
-            nc.vector.tensor_tensor(pre[:], un_ps[:], gated[:], ADD)
-            cand = work.tile([C, PIECE], F32, name="cand")
-            nc.scalar.activation(cand[:], pre[:], TANH, bias=bias_ih[:, 2:3])
-
             diff = work.tile([C, PIECE], F32, name="diff")
-            nc.vector.tensor_tensor(diff[:], own, cand[:], SUBTRACT)
+            nc.vector.tensor_tensor(diff[:], own[p], cand[p][:], SUBTRACT)
             step = work.tile([C, PIECE], F32, name="step")
-            nc.vector.tensor_tensor(step[:], z[:], diff[:], MULT)
+            nc.vector.tensor_tensor(step[:], z[p][:], diff[:], MULT)
             new = work.tile([C, PIECE], F32, name="new")
-            nc.vector.tensor_tensor(new[:], step[:], cand[:], ADD)
+            nc.vector.tensor_tensor(new[:], step[:], cand[p][:], ADD)
             nc.sync.dma_start(out[:, p * PIECE : (p + 1) * PIECE], new[:])

@@ -11,7 +11,6 @@ N = 1024
 PIECE = 512
 PIECES = N // PIECE
 LIST_COLS = PIECE // 16
-WARM_MATMULS = 4
 
 FLOPS = 2 * C * C * N + 2 * 2 * C * 3 * C * N
 
@@ -43,13 +42,10 @@ def tile_denseggnn_kernel(tc, x, w, w_ih, w_hh, b_ih, b_hh, offs, out):
         bias_rz = held.tile([C, 2], F32, name="bias_rz")
         nc.gpsimd.tensor_tensor(bias_rz[:], bias_ih[:, 0:2], bias_hh[:, 0:2], ADD)
 
-        zeros = held.tile([C, PIECE], BF16, name="zeros")
+        zeros = held.tile([C, 1], F32, name="zeros")
         nc.gpsimd.memset(zeros[:], 0.0)
-        idle_ps = turns.tile([C, PIECE], F32, name="idle_ps", tag="turn")
-        for i in range(WARM_MATMULS):
-            nc.tensor.matmul(idle_ps[:], zeros[:, 0:C], zeros[:], start=True, stop=True)
         idle_act = held.tile([C, 1], F32, name="idle_act")
-        nc.scalar.activation(idle_act[:], zeros[:, 0:1], SIGMOID)
+        nc.scalar.activation(idle_act[:], zeros[:], SIGMOID)
 
         own = [x_sb[:, p * PIECE : (p + 1) * PIECE] for p in range(PIECES)]
 

@@ -1,4 +1,5 @@
 import concourse.mybir as mybir
+from concourse.masks import make_identity
 
 BF16, F32, U16 = mybir.dt.bfloat16, mybir.dt.float32, mybir.dt.uint16
 ADD, SUBTRACT, MULT = mybir.AluOpType.add, mybir.AluOpType.subtract, mybir.AluOpType.mult
@@ -11,6 +12,7 @@ N = 1024
 PIECE = 512
 PIECES = N // PIECE
 LIST_COLS = PIECE // 16
+WARM_MATMULS = 4
 
 FLOPS = 2 * C * C * N + 2 * 2 * C * 3 * C * N
 
@@ -34,18 +36,27 @@ def tile_denseggnn_kernel(tc, x, w, w_ih, w_hh, b_ih, b_hh, offs, out):
         w_ih_sb = held.tile([C, 3 * C], BF16, name="w_ih_sb")
         nc.sync.dma_start(w_ih_sb[:], w_ih)
 
-        bias_ih = held.tile([C, 3], F32, name="bias_ih")
-        bias_hh = held.tile([C, 3], F32, name="bias_hh")
-        with nc.allow_non_contiguous_dma(reason="one bias value for each partition"):
-            nc.sync.dma_start(bias_ih[:], b_ih.rearrange("(g c) o -> c (g o)", c=C))
-            nc.sync.dma_start(bias_hh[:], b_hh.rearrange("(g c) o -> c (g o)", c=C))
-        bias_rz = held.tile([C, 2], F32, name="bias_rz")
-        nc.gpsimd.tensor_tensor(bias_rz[:], bias_ih[:, 0:2], bias_hh[:, 0:2], ADD)
+        bias_rows = held.tile([6, C], F32, name="bias_rows")
+        nc.sync.dma_start(bias_rows[0:3, :], b_ih.rearrange("(g c) o -> g (c o)", c=C))
+        nc.sync.dma_start(bias_rows[3:6, :], b_hh.rearrange("(g c) o -> g (c o)", c=C))
 
-        zeros = held.tile([C, 1], F32, name="zeros")
+        zeros = held.tile([C, PIECE], BF16, name="zeros")
         nc.gpsimd.memset(zeros[:], 0.0)
+        idle_ps = turns.tile([C, PIECE], F32, name="idle_ps", tag="turn")
+        for i in range(WARM_MATMULS):
+            nc.tensor.matmul(idle_ps[:], zeros[:, 0:C], zeros[:], start=True, stop=True)
         idle_act = held.tile([C, 1], F32, name="idle_act")
-        nc.scalar.activation(idle_act[:], zeros[:], SIGMOID)
+        nc.scalar.activation(idle_act[:], zeros[:, 0:1], SIGMOID)
+
+        identity = held.tile([6, 6], F32, name="identity")
+        make_identity(nc, identity[:])
+        bias_ps = turns.tile([C, 6], F32, name="bias_ps", tag="turn")
+        nc.tensor.matmul(bias_ps[:], bias_rows[:], identity[:], start=True, stop=True)
+        bias = held.tile([C, 6], F32, name="bias")
+        nc.vector.tensor_copy(bias[:], bias_ps[:])
+        bias_ih, bias_hh = bias[:, 0:3], bias[:, 3:6]
+        bias_rz = held.tile([C, 2], F32, name="bias_rz")
+        nc.vector.tensor_tensor(bias_rz[:], bias_ih[:, 0:2], bias_hh[:, 0:2], ADD)
 
         own = [x_sb[:, p * PIECE : (p + 1) * PIECE] for p in range(PIECES)]
 

@@ -1,5 +1,4 @@
 import concourse.mybir as mybir
-from concourse.masks import make_identity
 
 BF16, F32, U16 = mybir.dt.bfloat16, mybir.dt.float32, mybir.dt.uint16
 ADD, SUBTRACT, MULT = mybir.AluOpType.add, mybir.AluOpType.subtract, mybir.AluOpType.mult
@@ -12,7 +11,8 @@ N = 1024
 PIECE = 512
 PIECES = N // PIECE
 LIST_COLS = PIECE // 16
-WARM_MATMULS = 4
+CHUNK = PIECE // 2
+WARM_MATMULS = 16
 
 FLOPS = 2 * C * C * N + 2 * 2 * C * 3 * C * N
 
@@ -21,7 +21,7 @@ def tile_denseggnn_kernel(tc, x, w, w_ih, w_hh, b_ih, b_hh, offs, out):
     nc = tc.nc
     with (
         tc.tile_pool(name="held", bufs=1) as held,
-        tc.tile_pool(name="work", bufs=PIECES) as work,
+        tc.tile_pool(name="work", bufs=N // CHUNK) as work,
         tc.psum_pool(name="gates", bufs=PIECES) as gates,
         tc.psum_pool(name="turns", bufs=4) as turns,
     ):
@@ -34,29 +34,21 @@ def tile_denseggnn_kernel(tc, x, w, w_ih, w_hh, b_ih, b_hh, offs, out):
         w_hh_sb = held.tile([C, 3 * C], BF16, name="w_hh_sb")
         nc.scalar.dma_start(w_hh_sb[:], w_hh)
         w_ih_sb = held.tile([C, 3 * C], BF16, name="w_ih_sb")
-        nc.sync.dma_start(w_ih_sb[:], w_ih)
+        nc.scalar.dma_start(w_ih_sb[:], w_ih)
 
-        bias_rows = held.tile([6, C], F32, name="bias_rows")
-        nc.sync.dma_start(bias_rows[0:3, :], b_ih.rearrange("(g c) o -> g (c o)", c=C))
-        nc.sync.dma_start(bias_rows[3:6, :], b_hh.rearrange("(g c) o -> g (c o)", c=C))
+        bias_ih = held.tile([C, 3], F32, name="bias_ih")
+        bias_hh = held.tile([C, 3], F32, name="bias_hh")
+        with nc.allow_non_contiguous_dma(reason="one bias value for each partition"):
+            nc.sync.dma_start(bias_ih[:], b_ih.rearrange("(g c) o -> c (g o)", c=C))
+            nc.sync.dma_start(bias_hh[:], b_hh.rearrange("(g c) o -> c (g o)", c=C))
 
-        zeros = held.tile([C, PIECE], BF16, name="zeros")
-        nc.gpsimd.memset(zeros[:], 0.0)
-        idle_ps = turns.tile([C, PIECE], F32, name="idle_ps", tag="turn")
+        zeros = held.tile([C, C], BF16, name="zeros")
+        nc.vector.memset(zeros[:], 0.0)
+        idle_ps = turns.tile([C, C], F32, name="idle_ps", tag="turn")
         for i in range(WARM_MATMULS):
-            nc.tensor.matmul(idle_ps[:], zeros[:, 0:C], zeros[:], start=True, stop=True)
+            nc.tensor.matmul(idle_ps[:], zeros[:], zeros[:], start=True, stop=True)
         idle_act = held.tile([C, 1], F32, name="idle_act")
         nc.scalar.activation(idle_act[:], zeros[:, 0:1], SIGMOID)
-
-        identity = held.tile([6, 6], F32, name="identity")
-        make_identity(nc, identity[:])
-        bias_ps = turns.tile([C, 6], F32, name="bias_ps", tag="turn")
-        nc.tensor.matmul(bias_ps[:], bias_rows[:], identity[:], start=True, stop=True)
-        bias = held.tile([C, 6], F32, name="bias")
-        nc.vector.tensor_copy(bias[:], bias_ps[:])
-        bias_ih, bias_hh = bias[:, 0:3], bias[:, 3:6]
-        bias_rz = held.tile([C, 2], F32, name="bias_rz")
-        nc.vector.tensor_tensor(bias_rz[:], bias_ih[:, 0:2], bias_hh[:, 0:2], ADD)
 
         own = [x_sb[:, p * PIECE : (p + 1) * PIECE] for p in range(PIECES)]
 
@@ -70,6 +62,9 @@ def tile_denseggnn_kernel(tc, x, w, w_ih, w_hh, b_ih, b_hh, offs, out):
                 nc.vector.tensor_copy(m_bf[p][:], m_ps[:])
             else:
                 nc.scalar.activation(m_bf[p][:], m_ps[:], COPY)
+
+        bias_rz = held.tile([C, 2], F32, name="bias_rz")
+        nc.vector.tensor_tensor(bias_rz[:], bias_ih[:, 0:2], bias_hh[:, 0:2], ADD)
 
         r_ps, vn_ps, un_ps, z_ps = [], [], [], []
         for p in range(PIECES):
@@ -85,27 +80,39 @@ def tile_denseggnn_kernel(tc, x, w, w_ih, w_hh, b_ih, b_hh, offs, out):
             nc.tensor.matmul(z_ps[p][:], w_hh_sb[:, C : 2 * C], own[p], start=True, stop=False)
             nc.tensor.matmul(z_ps[p][:], w_ih_sb[:, C : 2 * C], m_bf[p][:], start=False, stop=True)
 
-        r = []
-        for p in range(PIECES):
-            r.append(work.tile([C, PIECE], F32, name="r"))
-            nc.scalar.activation(r[p][:], r_ps[p][:], SIGMOID, bias=bias_rz[:, 0:1])
+        def half(bank, c):
+            return bank[c // 2][:, (c % 2) * CHUNK : (c % 2 + 1) * CHUNK]
 
-        cand, z = [], []
-        for p in range(PIECES):
-            gated = work.tile([C, PIECE], F32, name="gated")
-            nc.vector.scalar_tensor_tensor(gated[:], vn_ps[p][:], bias_hh[:, 2:3], r[p][:], ADD, MULT)
-            pre = work.tile([C, PIECE], F32, name="pre")
-            nc.vector.tensor_tensor(pre[:], un_ps[p][:], gated[:], ADD)
-            cand.append(work.tile([C, PIECE], F32, name="cand"))
-            nc.scalar.activation(cand[p][:], pre[:], TANH, bias=bias_ih[:, 2:3])
-            z.append(work.tile([C, PIECE], F32, name="z"))
-            nc.scalar.activation(z[p][:], z_ps[p][:], SIGMOID, bias=bias_rz[:, 1:2])
+        pairs = [(2 * p, 2 * p + 1) for p in range(PIECES)]
+        r, gated, pre, cand, z, diff, step, new = {}, {}, {}, {}, {}, {}, {}, {}
 
-        for p in range(PIECES):
-            diff = work.tile([C, PIECE], F32, name="diff")
-            nc.vector.tensor_tensor(diff[:], own[p], cand[p][:], SUBTRACT)
-            step = work.tile([C, PIECE], F32, name="step")
-            nc.vector.tensor_tensor(step[:], z[p][:], diff[:], MULT)
-            new = work.tile([C, PIECE], F32, name="new")
-            nc.vector.tensor_tensor(new[:], step[:], cand[p][:], ADD)
-            nc.sync.dma_start(out[:, p * PIECE : (p + 1) * PIECE], new[:])
+        for pair in pairs:
+            for c in pair:
+                r[c] = work.tile([C, CHUNK], F32, name="r")
+                nc.scalar.activation(r[c][:], half(r_ps, c), SIGMOID, bias=bias_rz[:, 0:1])
+
+        for pair in pairs:
+            for c in pair:
+                gated[c] = work.tile([C, CHUNK], F32, name="gated")
+                nc.vector.scalar_tensor_tensor(gated[c][:], half(vn_ps, c), bias_hh[:, 2:3], r[c][:], ADD, MULT)
+            for c in pair:
+                pre[c] = work.tile([C, CHUNK], F32, name="pre")
+                nc.vector.tensor_tensor(pre[c][:], half(un_ps, c), gated[c][:], ADD)
+            for c in pair:
+                cand[c] = work.tile([C, CHUNK], F32, name="cand")
+                nc.scalar.activation(cand[c][:], pre[c][:], TANH, bias=bias_ih[:, 2:3])
+            for c in pair:
+                z[c] = work.tile([C, CHUNK], F32, name="z")
+                nc.scalar.activation(z[c][:], half(z_ps, c), SIGMOID, bias=bias_rz[:, 1:2])
+
+        for pair in pairs:
+            for c in pair:
+                diff[c] = work.tile([C, CHUNK], F32, name="diff")
+                nc.vector.tensor_tensor(diff[c][:], x_sb[:, c * CHUNK : (c + 1) * CHUNK], cand[c][:], SUBTRACT)
+            for c in pair:
+                step[c] = work.tile([C, CHUNK], F32, name="step")
+                nc.vector.tensor_tensor(step[c][:], z[c][:], diff[c][:], MULT)
+            for c in pair:
+                new[c] = work.tile([C, CHUNK], F32, name="new")
+                nc.vector.tensor_tensor(new[c][:], step[c][:], cand[c][:], ADD)
+                nc.sync.dma_start(out[:, c * CHUNK : (c + 1) * CHUNK], new[c][:])

@@ -1,4 +1,5 @@
 import concourse.mybir as mybir
+from concourse.masks import make_identity
 
 BF16, F32, U16 = mybir.dt.bfloat16, mybir.dt.float32, mybir.dt.uint16
 ADD, SUBTRACT, MULT = mybir.AluOpType.add, mybir.AluOpType.subtract, mybir.AluOpType.mult
@@ -10,8 +11,9 @@ S = 1024
 N = 1024
 PIECE = 512
 PIECES = N // PIECE
-LIST_COLS = PIECE // 16
 CHUNK = PIECE // 2
+CHUNKS = N // CHUNK
+LIST_COLS = CHUNK // 16
 WARM_MATMULS = 16
 
 FLOPS = 2 * C * C * N + 2 * 2 * C * 3 * C * N
@@ -21,7 +23,7 @@ def tile_denseggnn_kernel(tc, x, w, w_ih, w_hh, b_ih, b_hh, offs, out):
     nc = tc.nc
     with (
         tc.tile_pool(name="held", bufs=1) as held,
-        tc.tile_pool(name="work", bufs=N // CHUNK) as work,
+        tc.tile_pool(name="work", bufs=CHUNKS) as work,
         tc.psum_pool(name="gates", bufs=PIECES) as gates,
         tc.psum_pool(name="turns", bufs=4) as turns,
     ):
@@ -50,18 +52,21 @@ def tile_denseggnn_kernel(tc, x, w, w_ih, w_hh, b_ih, b_hh, offs, out):
         idle_act = held.tile([C, 1], F32, name="idle_act")
         nc.scalar.activation(idle_act[:], zeros[:, 0:1], SIGMOID)
 
+        ident = held.tile([C, C], F32, name="ident")
+        make_identity(nc, ident[:])
+
         own = [x_sb[:, p * PIECE : (p + 1) * PIECE] for p in range(PIECES)]
 
-        m_bf = []
-        for p in range(PIECES):
-            m_ps = turns.tile([C, PIECE], F32, name=f"m_ps{p}", tag="turn")
-            picked = x_sb[:].indirect(offsets[:, p * LIST_COLS : (p + 1) * LIST_COLS])
+        m_bf = [held.tile([C, PIECE], BF16, name=f"m_bf{p}") for p in range(PIECES)]
+        for c in range(CHUNKS):
+            m_ps = turns.tile([C, CHUNK], F32, name=f"m_ps{c}", tag="turn")
+            picked = x_sb[:].indirect(offsets[:, c * LIST_COLS : (c + 1) * LIST_COLS])
             nc.tensor.matmul(m_ps[:], w_sb[:], picked, start=True, stop=True)
-            m_bf.append(held.tile([C, PIECE], BF16, name=f"m_bf{p}"))
-            if p % 2 == 0:
-                nc.vector.tensor_copy(m_bf[p][:], m_ps[:])
+            m_chunk = m_bf[c // 2][:, (c % 2) * CHUNK : (c % 2 + 1) * CHUNK]
+            if c % 2 == 0:
+                nc.vector.tensor_copy(m_chunk, m_ps[:])
             else:
-                nc.scalar.activation(m_bf[p][:], m_ps[:], COPY)
+                nc.scalar.activation(m_chunk, m_ps[:], COPY)
 
         bias_rz = held.tile([C, 2], F32, name="bias_rz")
         nc.vector.tensor_tensor(bias_rz[:], bias_ih[:, 0:2], bias_hh[:, 0:2], ADD)
@@ -74,7 +79,8 @@ def tile_denseggnn_kernel(tc, x, w, w_ih, w_hh, b_ih, b_hh, offs, out):
             vn_ps.append(turns.tile([C, PIECE], F32, name=f"vn_ps{p}", tag="turn"))
             nc.tensor.matmul(vn_ps[p][:], w_hh_sb[:, 2 * C : 3 * C], own[p], start=True, stop=True)
             un_ps.append(turns.tile([C, PIECE], F32, name=f"un_ps{p}", tag="turn"))
-            nc.tensor.matmul(un_ps[p][:], w_ih_sb[:, 2 * C : 3 * C], m_bf[p][:], start=True, stop=True)
+            nc.tensor.matmul(un_ps[p][:, 0:CHUNK], w_ih_sb[:, 2 * C : 3 * C], m_bf[p][:, 0:CHUNK], start=True, stop=True)
+            nc.tensor.matmul(un_ps[p][:, CHUNK:PIECE], w_ih_sb[:, 2 * C : 3 * C], m_bf[p][:, CHUNK:PIECE], start=True, stop=False)
         for p in range(PIECES):
             z_ps.append(gates.tile([C, PIECE], F32, name="z_ps"))
             nc.tensor.matmul(z_ps[p][:], w_hh_sb[:, C : 2 * C], own[p], start=True, stop=False)
@@ -84,7 +90,7 @@ def tile_denseggnn_kernel(tc, x, w, w_ih, w_hh, b_ih, b_hh, offs, out):
             return bank[c // 2][:, (c % 2) * CHUNK : (c % 2 + 1) * CHUNK]
 
         pairs = [(2 * p, 2 * p + 1) for p in range(PIECES)]
-        r, gated, pre, cand, z, diff, step, new = {}, {}, {}, {}, {}, {}, {}, {}
+        r, gated, pre, cand, z, kept, step, new = {}, {}, {}, {}, {}, {}, {}, {}
 
         for pair in pairs:
             for c in pair:
@@ -95,24 +101,26 @@ def tile_denseggnn_kernel(tc, x, w, w_ih, w_hh, b_ih, b_hh, offs, out):
             for c in pair:
                 gated[c] = work.tile([C, CHUNK], F32, name="gated")
                 nc.vector.scalar_tensor_tensor(gated[c][:], half(vn_ps, c), bias_hh[:, 2:3], r[c][:], ADD, MULT)
-            for c in pair:
-                pre[c] = work.tile([C, CHUNK], F32, name="pre")
-                nc.vector.tensor_tensor(pre[c][:], half(un_ps, c), gated[c][:], ADD)
-            for c in pair:
+            even, odd = pair
+            pre[even] = work.tile([C, CHUNK], F32, name="pre")
+            nc.vector.tensor_tensor(pre[even][:], half(un_ps, even), gated[even][:], ADD)
+            nc.tensor.matmul(half(un_ps, odd), ident[:], gated[odd][:], start=False, stop=True)
+            for c, summed in ((even, pre[even][:]), (odd, half(un_ps, odd))):
                 cand[c] = work.tile([C, CHUNK], F32, name="cand")
-                nc.scalar.activation(cand[c][:], pre[c][:], TANH, bias=bias_ih[:, 2:3])
+                nc.scalar.activation(cand[c][:], summed, TANH, bias=bias_ih[:, 2:3])
             for c in pair:
                 z[c] = work.tile([C, CHUNK], F32, name="z")
                 nc.scalar.activation(z[c][:], half(z_ps, c), SIGMOID, bias=bias_rz[:, 1:2])
 
         for pair in pairs:
             for c in pair:
-                diff[c] = work.tile([C, CHUNK], F32, name="diff")
-                nc.vector.tensor_tensor(diff[c][:], x_sb[:, c * CHUNK : (c + 1) * CHUNK], cand[c][:], SUBTRACT)
+                kept[c] = work.tile([C, CHUNK], F32, name="kept")
+                nc.vector.tensor_tensor(kept[c][:], z[c][:], x_sb[:, c * CHUNK : (c + 1) * CHUNK], MULT)
+        for pair in pairs:
             for c in pair:
                 step[c] = work.tile([C, CHUNK], F32, name="step")
-                nc.vector.tensor_tensor(step[c][:], z[c][:], diff[c][:], MULT)
+                nc.vector.scalar_tensor_tensor(step[c][:], z[c][:], 1.0, cand[c][:], SUBTRACT, MULT)
             for c in pair:
                 new[c] = work.tile([C, CHUNK], F32, name="new")
-                nc.vector.tensor_tensor(new[c][:], step[c][:], cand[c][:], ADD)
+                nc.vector.tensor_tensor(new[c][:], kept[c][:], step[c][:], SUBTRACT)
                 nc.sync.dma_start(out[:, c * CHUNK : (c + 1) * CHUNK], new[c][:])

@@ -71,56 +71,51 @@ def tile_denseggnn_kernel(tc, x, w, w_ih, w_hh, b_ih, b_hh, offs, out):
         bias_rz = held.tile([C, 2], F32, name="bias_rz")
         nc.vector.tensor_tensor(bias_rz[:], bias_ih[:, 0:2], bias_hh[:, 0:2], ADD)
 
-        r_ps, vn_ps, un_ps, z_ps = [], [], [], []
+        halves = [slice(h * CHUNK, (h + 1) * CHUNK) for h in range(2)]
+        un_ps, z_ps, pre, cand, z = [], [], [], [], []
+
         for p in range(PIECES):
-            r_ps.append(gates.tile([C, PIECE], F32, name="r_ps"))
-            nc.tensor.matmul(r_ps[p][:], w_hh_sb[:, 0:C], own[p], start=True, stop=False)
-            nc.tensor.matmul(r_ps[p][:], w_ih_sb[:, 0:C], m_bf[p][:], start=False, stop=True)
-            vn_ps.append(turns.tile([C, PIECE], F32, name=f"vn_ps{p}", tag="turn"))
-            nc.tensor.matmul(vn_ps[p][:], w_hh_sb[:, 2 * C : 3 * C], own[p], start=True, stop=True)
-            un_ps.append(turns.tile([C, PIECE], F32, name=f"un_ps{p}", tag="turn"))
-            nc.tensor.matmul(un_ps[p][:, 0:CHUNK], w_ih_sb[:, 2 * C : 3 * C], m_bf[p][:, 0:CHUNK], start=True, stop=True)
-            nc.tensor.matmul(un_ps[p][:, CHUNK:PIECE], w_ih_sb[:, 2 * C : 3 * C], m_bf[p][:, CHUNK:PIECE], start=True, stop=False)
-        for p in range(PIECES):
+            r_ps = gates.tile([C, PIECE], F32, name="r_ps")
+            nc.tensor.matmul(r_ps[:], w_hh_sb[:, 0:C], own[p], start=True, stop=False)
+            nc.tensor.matmul(r_ps[:], w_ih_sb[:, 0:C], m_bf[p][:], start=False, stop=True)
+            vn_ps = turns.tile([C, PIECE], F32, name=f"vn_ps{p}", tag="turn")
+            nc.tensor.matmul(vn_ps[:], w_hh_sb[:, 2 * C : 3 * C], own[p], start=True, stop=True)
             z_ps.append(gates.tile([C, PIECE], F32, name="z_ps"))
             nc.tensor.matmul(z_ps[p][:], w_hh_sb[:, C : 2 * C], own[p], start=True, stop=False)
             nc.tensor.matmul(z_ps[p][:], w_ih_sb[:, C : 2 * C], m_bf[p][:], start=False, stop=True)
+            un_ps.append(turns.tile([C, PIECE], F32, name=f"un_ps{p}", tag="turn"))
+            for h, complete in zip(halves, (True, False)):
+                nc.tensor.matmul(un_ps[p][:, h], w_ih_sb[:, 2 * C : 3 * C], m_bf[p][:, h], start=True, stop=complete)
 
-        def half(bank, c):
-            return bank[c // 2][:, (c % 2) * CHUNK : (c % 2 + 1) * CHUNK]
+            r, gated = [], []
+            for h in halves:
+                r.append(work.tile([C, CHUNK], F32, name="r"))
+                nc.scalar.activation(r[-1][:], r_ps[:, h], SIGMOID, bias=bias_rz[:, 0:1])
+            for i, h in enumerate(halves):
+                gated.append(work.tile([C, CHUNK], F32, name="gated"))
+                nc.vector.scalar_tensor_tensor(gated[i][:], vn_ps[:, h], bias_hh[:, 2:3], r[i][:], ADD, MULT)
+            pre.append(work.tile([C, CHUNK], F32, name="pre"))
+            nc.vector.tensor_tensor(pre[p][:], un_ps[p][:, halves[0]], gated[0][:], ADD)
+            nc.tensor.matmul(un_ps[p][:, halves[1]], ident[:], gated[1][:], start=False, stop=True)
 
-        pairs = [(2 * p, 2 * p + 1) for p in range(PIECES)]
-        r, gated, pre, cand, z, kept, step, new = {}, {}, {}, {}, {}, {}, {}, {}
+        for p in range(PIECES):
+            for summed in (pre[p][:], un_ps[p][:, halves[1]]):
+                cand.append(work.tile([C, CHUNK], F32, name="cand"))
+                nc.scalar.activation(cand[-1][:], summed, TANH, bias=bias_ih[:, 2:3])
+            for h in halves:
+                z.append(work.tile([C, CHUNK], F32, name="z"))
+                nc.scalar.activation(z[-1][:], z_ps[p][:, h], SIGMOID, bias=bias_rz[:, 1:2])
 
-        for pair in pairs:
-            for c in pair:
-                r[c] = work.tile([C, CHUNK], F32, name="r")
-                nc.scalar.activation(r[c][:], half(r_ps, c), SIGMOID, bias=bias_rz[:, 0:1])
-
-        for pair in pairs:
-            for c in pair:
-                gated[c] = work.tile([C, CHUNK], F32, name="gated")
-                nc.vector.scalar_tensor_tensor(gated[c][:], half(vn_ps, c), bias_hh[:, 2:3], r[c][:], ADD, MULT)
-            even, odd = pair
-            pre[even] = work.tile([C, CHUNK], F32, name="pre")
-            nc.vector.tensor_tensor(pre[even][:], half(un_ps, even), gated[even][:], ADD)
-            nc.tensor.matmul(half(un_ps, odd), ident[:], gated[odd][:], start=False, stop=True)
-            for c, summed in ((even, pre[even][:]), (odd, half(un_ps, odd))):
-                cand[c] = work.tile([C, CHUNK], F32, name="cand")
-                nc.scalar.activation(cand[c][:], summed, TANH, bias=bias_ih[:, 2:3])
-            for c in pair:
-                z[c] = work.tile([C, CHUNK], F32, name="z")
-                nc.scalar.activation(z[c][:], half(z_ps, c), SIGMOID, bias=bias_rz[:, 1:2])
-
-        for pair in pairs:
-            for c in pair:
+        for p in range(PIECES):
+            chunks = (2 * p, 2 * p + 1)
+            kept, step = {}, {}
+            for c in chunks:
                 kept[c] = work.tile([C, CHUNK], F32, name="kept")
                 nc.vector.tensor_tensor(kept[c][:], z[c][:], x_sb[:, c * CHUNK : (c + 1) * CHUNK], MULT)
-        for pair in pairs:
-            for c in pair:
+            for c in chunks:
                 step[c] = work.tile([C, CHUNK], F32, name="step")
                 nc.vector.scalar_tensor_tensor(step[c][:], z[c][:], 1.0, cand[c][:], SUBTRACT, MULT)
-            for c in pair:
-                new[c] = work.tile([C, CHUNK], F32, name="new")
-                nc.vector.tensor_tensor(new[c][:], kept[c][:], step[c][:], SUBTRACT)
-                nc.sync.dma_start(out[:, c * CHUNK : (c + 1) * CHUNK], new[c][:])
+            for c in chunks:
+                new = work.tile([C, CHUNK], F32, name="new")
+                nc.vector.tensor_tensor(new[:], kept[c][:], step[c][:], SUBTRACT)
+                nc.sync.dma_start(out[:, c * CHUNK : (c + 1) * CHUNK], new[:])

@@ -14,6 +14,7 @@ PIECES = N // PIECE
 CHUNK = PIECE // 2
 CHUNKS = N // CHUNK
 LIST_COLS = CHUNK // 16
+PSUM_BANKS = 8
 WARM_MATMULS = 16
 
 FLOPS = 2 * C * C * N + 2 * 2 * C * 3 * C * N
@@ -24,8 +25,7 @@ def tile_denseggnn_kernel(tc, x, w, w_ih, w_hh, b_ih, b_hh, offs, out):
     with (
         tc.tile_pool(name="held", bufs=1) as held,
         tc.tile_pool(name="work", bufs=CHUNKS) as work,
-        tc.psum_pool(name="gates", bufs=PIECES) as gates,
-        tc.psum_pool(name="turns", bufs=4) as turns,
+        tc.psum_pool(name="banks", bufs=PSUM_BANKS) as banks,
     ):
         offsets = held.tile([C, N // 16], U16, name="offsets")
         nc.sync.dma_start(offsets[:], offs)
@@ -46,7 +46,7 @@ def tile_denseggnn_kernel(tc, x, w, w_ih, w_hh, b_ih, b_hh, offs, out):
 
         zeros = held.tile([C, C], BF16, name="zeros")
         nc.vector.memset(zeros[:], 0.0)
-        idle_ps = turns.tile([C, C], F32, name="idle_ps", tag="turn")
+        idle_ps = banks.tile([C, C], F32, name="idle_ps", tag="bank")
         for i in range(WARM_MATMULS):
             nc.tensor.matmul(idle_ps[:], zeros[:], zeros[:], start=True, stop=True)
         idle_act = held.tile([C, 1], F32, name="idle_act")
@@ -59,7 +59,7 @@ def tile_denseggnn_kernel(tc, x, w, w_ih, w_hh, b_ih, b_hh, offs, out):
 
         m_bf = [held.tile([C, PIECE], BF16, name=f"m_bf{p}") for p in range(PIECES)]
         for c in range(CHUNKS):
-            m_ps = turns.tile([C, CHUNK], F32, name=f"m_ps{c}", tag="turn")
+            m_ps = banks.tile([C, CHUNK], F32, name=f"m_ps{c}", tag="bank")
             picked = x_sb[:].indirect(offsets[:, c * LIST_COLS : (c + 1) * LIST_COLS])
             nc.tensor.matmul(m_ps[:], w_sb[:], picked, start=True, stop=True)
             m_chunk = m_bf[c // 2][:, (c % 2) * CHUNK : (c % 2 + 1) * CHUNK]
@@ -72,20 +72,21 @@ def tile_denseggnn_kernel(tc, x, w, w_ih, w_hh, b_ih, b_hh, offs, out):
         nc.vector.tensor_tensor(bias_rz[:], bias_ih[:, 0:2], bias_hh[:, 0:2], ADD)
 
         halves = [slice(h * CHUNK, (h + 1) * CHUNK) for h in range(2)]
-        un_ps, z_ps, pre, cand, z = [], [], [], [], []
+        un_open, z_ps, pre, cand, z = [], [], [], [], []
 
         for p in range(PIECES):
-            r_ps = gates.tile([C, PIECE], F32, name="r_ps")
+            r_ps = banks.tile([C, PIECE], F32, name=f"r_ps{p}", tag="bank")
             nc.tensor.matmul(r_ps[:], w_hh_sb[:, 0:C], own[p], start=True, stop=False)
             nc.tensor.matmul(r_ps[:], w_ih_sb[:, 0:C], m_bf[p][:], start=False, stop=True)
-            vn_ps = turns.tile([C, PIECE], F32, name=f"vn_ps{p}", tag="turn")
+            vn_ps = banks.tile([C, PIECE], F32, name=f"vn_ps{p}", tag="bank")
             nc.tensor.matmul(vn_ps[:], w_hh_sb[:, 2 * C : 3 * C], own[p], start=True, stop=True)
-            z_ps.append(gates.tile([C, PIECE], F32, name="z_ps"))
+            z_ps.append(banks.tile([C, PIECE], F32, name=f"z_ps{p}", tag="bank"))
             nc.tensor.matmul(z_ps[p][:], w_hh_sb[:, C : 2 * C], own[p], start=True, stop=False)
             nc.tensor.matmul(z_ps[p][:], w_ih_sb[:, C : 2 * C], m_bf[p][:], start=False, stop=True)
-            un_ps.append(turns.tile([C, PIECE], F32, name=f"un_ps{p}", tag="turn"))
-            for h, complete in zip(halves, (True, False)):
-                nc.tensor.matmul(un_ps[p][:, h], w_ih_sb[:, 2 * C : 3 * C], m_bf[p][:, h], start=True, stop=complete)
+            un_done = banks.tile([C, CHUNK], F32, name=f"un_done{p}", tag="bank")
+            nc.tensor.matmul(un_done[:], w_ih_sb[:, 2 * C : 3 * C], m_bf[p][:, halves[0]], start=True, stop=True)
+            un_open.append(banks.tile([C, CHUNK], F32, name=f"un_open{p}", tag="bank"))
+            nc.tensor.matmul(un_open[p][:], w_ih_sb[:, 2 * C : 3 * C], m_bf[p][:, halves[1]], start=True, stop=False)
 
             r, gated = [], []
             for h in halves:
@@ -95,11 +96,11 @@ def tile_denseggnn_kernel(tc, x, w, w_ih, w_hh, b_ih, b_hh, offs, out):
                 gated.append(work.tile([C, CHUNK], F32, name="gated"))
                 nc.vector.scalar_tensor_tensor(gated[i][:], vn_ps[:, h], bias_hh[:, 2:3], r[i][:], ADD, MULT)
             pre.append(work.tile([C, CHUNK], F32, name="pre"))
-            nc.vector.tensor_tensor(pre[p][:], un_ps[p][:, halves[0]], gated[0][:], ADD)
-            nc.tensor.matmul(un_ps[p][:, halves[1]], ident[:], gated[1][:], start=False, stop=True)
+            nc.vector.tensor_tensor(pre[p][:], un_done[:], gated[0][:], ADD)
+            nc.tensor.matmul(un_open[p][:], ident[:], gated[1][:], start=False, stop=True)
 
         for p in range(PIECES):
-            for summed in (pre[p][:], un_ps[p][:, halves[1]]):
+            for summed in (pre[p][:], un_open[p][:]):
                 cand.append(work.tile([C, CHUNK], F32, name="cand"))
                 nc.scalar.activation(cand[-1][:], summed, TANH, bias=bias_ih[:, 2:3])
             for h in halves:

@@ -9,9 +9,7 @@ COPY = mybir.ActivationFunctionType.Copy
 C = 128
 S = 1024
 N = 1024
-PIECE = 512
-PIECES = N // PIECE
-CHUNK = PIECE // 2
+CHUNK = 256
 CHUNKS = N // CHUNK
 LIST_COLS = CHUNK // 16
 PSUM_BANKS = 8
@@ -55,68 +53,61 @@ def tile_denseggnn_kernel(tc, x, w, w_ih, w_hh, b_ih, b_hh, offs, out):
         ident = held.tile([C, C], F32, name="ident")
         make_identity(nc, ident[:])
 
-        own = [x_sb[:, p * PIECE : (p + 1) * PIECE] for p in range(PIECES)]
+        own = [x_sb[:, c * CHUNK : (c + 1) * CHUNK] for c in range(CHUNKS)]
 
-        m_bf = [held.tile([C, PIECE], BF16, name=f"m_bf{p}") for p in range(PIECES)]
+        m_bf = [held.tile([C, CHUNK], BF16, name=f"m_bf{c}") for c in range(CHUNKS)]
         for c in range(CHUNKS):
             m_ps = banks.tile([C, CHUNK], F32, name=f"m_ps{c}", tag="bank")
             picked = x_sb[:].indirect(offsets[:, c * LIST_COLS : (c + 1) * LIST_COLS])
             nc.tensor.matmul(m_ps[:], w_sb[:], picked, start=True, stop=True)
-            m_chunk = m_bf[c // 2][:, (c % 2) * CHUNK : (c % 2 + 1) * CHUNK]
             if c % 2 == 0:
-                nc.vector.tensor_copy(m_chunk, m_ps[:])
+                nc.vector.tensor_copy(m_bf[c][:], m_ps[:])
             else:
-                nc.scalar.activation(m_chunk, m_ps[:], COPY)
+                nc.scalar.activation(m_bf[c][:], m_ps[:], COPY)
 
         bias_rz = held.tile([C, 2], F32, name="bias_rz")
         nc.vector.tensor_tensor(bias_rz[:], bias_ih[:, 0:2], bias_hh[:, 0:2], ADD)
 
-        halves = [slice(h * CHUNK, (h + 1) * CHUNK) for h in range(2)]
-        un_open, z_ps, pre, cand, z = [], [], [], [], []
+        w_r, w_z, w_n = slice(0, C), slice(C, 2 * C), slice(2 * C, 3 * C)
+        gated, z, summed = {}, {}, {}
 
-        for p in range(PIECES):
-            r_ps = banks.tile([C, PIECE], F32, name=f"r_ps{p}", tag="bank")
-            nc.tensor.matmul(r_ps[:], w_hh_sb[:, 0:C], own[p], start=True, stop=False)
-            nc.tensor.matmul(r_ps[:], w_ih_sb[:, 0:C], m_bf[p][:], start=False, stop=True)
-            vn_ps = banks.tile([C, PIECE], F32, name=f"vn_ps{p}", tag="bank")
-            nc.tensor.matmul(vn_ps[:], w_hh_sb[:, 2 * C : 3 * C], own[p], start=True, stop=True)
-            z_ps.append(banks.tile([C, PIECE], F32, name=f"z_ps{p}", tag="bank"))
-            nc.tensor.matmul(z_ps[p][:], w_hh_sb[:, C : 2 * C], own[p], start=True, stop=False)
-            nc.tensor.matmul(z_ps[p][:], w_ih_sb[:, C : 2 * C], m_bf[p][:], start=False, stop=True)
-            un_done = banks.tile([C, CHUNK], F32, name=f"un_done{p}", tag="bank")
-            nc.tensor.matmul(un_done[:], w_ih_sb[:, 2 * C : 3 * C], m_bf[p][:, halves[0]], start=True, stop=True)
-            un_open.append(banks.tile([C, CHUNK], F32, name=f"un_open{p}", tag="bank"))
-            nc.tensor.matmul(un_open[p][:], w_ih_sb[:, 2 * C : 3 * C], m_bf[p][:, halves[1]], start=True, stop=False)
+        for ahead in range(CHUNKS + 1):
+            behind = ahead - 1
+            if ahead < CHUNKS:
+                c = ahead
+                r_ps = banks.tile([C, CHUNK], F32, name=f"r_ps{c}", tag="bank")
+                nc.tensor.matmul(r_ps[:], w_hh_sb[:, w_r], own[c], start=True, stop=False)
+                nc.tensor.matmul(r_ps[:], w_ih_sb[:, w_r], m_bf[c][:], start=False, stop=True)
+                vn_ps = banks.tile([C, CHUNK], F32, name=f"vn_ps{c}", tag="bank")
+                nc.tensor.matmul(vn_ps[:], w_hh_sb[:, w_n], own[c], start=True, stop=True)
+                r = work.tile([C, CHUNK], F32, name="r")
+                nc.scalar.activation(r[:], r_ps[:], SIGMOID, bias=bias_rz[:, 0:1])
+                gated[c] = work.tile([C, CHUNK], F32, name="gated")
+                nc.vector.scalar_tensor_tensor(gated[c][:], vn_ps[:], bias_hh[:, 2:3], r[:], ADD, MULT)
+            if behind >= 0:
+                c = behind
+                z_ps = banks.tile([C, CHUNK], F32, name=f"z_ps{c}", tag="bank")
+                nc.tensor.matmul(z_ps[:], w_hh_sb[:, w_z], own[c], start=True, stop=False)
+                nc.tensor.matmul(z_ps[:], w_ih_sb[:, w_z], m_bf[c][:], start=False, stop=True)
+                z[c] = work.tile([C, CHUNK], F32, name="z")
+                nc.scalar.activation(z[c][:], z_ps[:], SIGMOID, bias=bias_rz[:, 1:2])
+                on_vector = c % 2 == 0
+                un_ps = banks.tile([C, CHUNK], F32, name=f"un_ps{c}", tag="bank")
+                nc.tensor.matmul(un_ps[:], w_ih_sb[:, w_n], m_bf[c][:], start=True, stop=on_vector)
+                if on_vector:
+                    summed[c] = work.tile([C, CHUNK], F32, name="pre")
+                    nc.vector.tensor_tensor(summed[c][:], un_ps[:], gated[c][:], ADD)
+                else:
+                    nc.tensor.matmul(un_ps[:], ident[:], gated[c][:], start=False, stop=True)
+                    summed[c] = un_ps
 
-            r, gated = [], []
-            for h in halves:
-                r.append(work.tile([C, CHUNK], F32, name="r"))
-                nc.scalar.activation(r[-1][:], r_ps[:, h], SIGMOID, bias=bias_rz[:, 0:1])
-            for i, h in enumerate(halves):
-                gated.append(work.tile([C, CHUNK], F32, name="gated"))
-                nc.vector.scalar_tensor_tensor(gated[i][:], vn_ps[:, h], bias_hh[:, 2:3], r[i][:], ADD, MULT)
-            pre.append(work.tile([C, CHUNK], F32, name="pre"))
-            nc.vector.tensor_tensor(pre[p][:], un_done[:], gated[0][:], ADD)
-            nc.tensor.matmul(un_open[p][:], ident[:], gated[1][:], start=False, stop=True)
-
-        for p in range(PIECES):
-            for summed in (pre[p][:], un_open[p][:]):
-                cand.append(work.tile([C, CHUNK], F32, name="cand"))
-                nc.scalar.activation(cand[-1][:], summed, TANH, bias=bias_ih[:, 2:3])
-            for h in halves:
-                z.append(work.tile([C, CHUNK], F32, name="z"))
-                nc.scalar.activation(z[-1][:], z_ps[p][:, h], SIGMOID, bias=bias_rz[:, 1:2])
-
-        for p in range(PIECES):
-            chunks = (2 * p, 2 * p + 1)
-            kept, step = {}, {}
-            for c in chunks:
-                kept[c] = work.tile([C, CHUNK], F32, name="kept")
-                nc.vector.tensor_tensor(kept[c][:], z[c][:], x_sb[:, c * CHUNK : (c + 1) * CHUNK], MULT)
-            for c in chunks:
-                step[c] = work.tile([C, CHUNK], F32, name="step")
-                nc.vector.scalar_tensor_tensor(step[c][:], z[c][:], 1.0, cand[c][:], SUBTRACT, MULT)
-            for c in chunks:
-                new = work.tile([C, CHUNK], F32, name="new")
-                nc.vector.tensor_tensor(new[:], kept[c][:], step[c][:], SUBTRACT)
-                nc.sync.dma_start(out[:, c * CHUNK : (c + 1) * CHUNK], new[:])
+        for c in range(CHUNKS):
+            cand = work.tile([C, CHUNK], F32, name="cand")
+            nc.scalar.activation(cand[:], summed[c][:], TANH, bias=bias_ih[:, 2:3])
+            kept = work.tile([C, CHUNK], F32, name="kept")
+            nc.vector.tensor_tensor(kept[:], z[c][:], own[c], MULT)
+            step = work.tile([C, CHUNK], F32, name="step")
+            nc.vector.scalar_tensor_tensor(step[:], z[c][:], 1.0, cand[:], SUBTRACT, MULT)
+            new = work.tile([C, CHUNK], F32, name="new")
+            nc.vector.tensor_tensor(new[:], kept[:], step[:], SUBTRACT)
+            nc.sync.dma_start(out[:, c * CHUNK : (c + 1) * CHUNK], new[:])

@@ -91,7 +91,7 @@ def tile_denseggnn_kernel(tc, x, w, w_ih, w_hh, b_ih, b_hh, offs, out):
                 nc.tensor.matmul(z_ps[:], w_ih_sb[:, w_z], m_bf[c][:], start=False, stop=True)
                 z[c] = work.tile([C, CHUNK], F32, name="z")
                 nc.scalar.activation(z[c][:], z_ps[:], SIGMOID, bias=bias_rz[:, 1:2])
-                on_vector = c % 2 == 0
+                on_vector = c == 0
                 un_ps = banks.tile([C, CHUNK], F32, name=f"un_ps{c}", tag="bank")
                 nc.tensor.matmul(un_ps[:], w_ih_sb[:, w_n], m_bf[c][:], start=True, stop=on_vector)
                 if on_vector:

@@ -11,7 +11,7 @@ S = 1024
 N = 1024
 CHUNK = 256
 CHUNKS = N // CHUNK
-LIST_COLS = CHUNK // 16
+PIECE = 512
 PSUM_BANKS = 8
 WARM_MATMULS = 16
 
@@ -56,14 +56,16 @@ def tile_denseggnn_kernel(tc, x, w, w_ih, w_hh, b_ih, b_hh, offs, out):
         own = [x_sb[:, c * CHUNK : (c + 1) * CHUNK] for c in range(CHUNKS)]
 
         m_bf = [held.tile([C, CHUNK], BF16, name=f"m_bf{c}") for c in range(CHUNKS)]
-        for c in range(CHUNKS):
-            m_ps = banks.tile([C, CHUNK], F32, name=f"m_ps{c}", tag="bank")
-            picked = x_sb[:].indirect(offsets[:, c * LIST_COLS : (c + 1) * LIST_COLS])
+        for p in range(N // PIECE):
+            m_ps = banks.tile([C, PIECE], F32, name=f"m_ps{p}", tag="bank")
+            picked = x_sb[:].indirect(offsets[:, p * (PIECE // 16) : (p + 1) * (PIECE // 16)])
             nc.tensor.matmul(m_ps[:], w_sb[:], picked, start=True, stop=True)
-            if c % 2 == 0:
-                nc.vector.tensor_copy(m_bf[c][:], m_ps[:])
-            else:
-                nc.scalar.activation(m_bf[c][:], m_ps[:], COPY)
+            for half in range(PIECE // CHUNK):
+                c = p * (PIECE // CHUNK) + half
+                if p % 2 == 0:
+                    nc.vector.tensor_copy(m_bf[c][:], m_ps[:, half * CHUNK : (half + 1) * CHUNK])
+                else:
+                    nc.scalar.activation(m_bf[c][:], m_ps[:, half * CHUNK : (half + 1) * CHUNK], COPY)
 
         bias_rz = held.tile([C, 2], F32, name="bias_rz")
         nc.vector.tensor_tensor(bias_rz[:], bias_ih[:, 0:2], bias_hh[:, 0:2], ADD)

import concourse.mybir as mybir
from concourse.masks import make_identity

BF16, F32, U16 = mybir.dt.bfloat16, mybir.dt.float32, mybir.dt.uint16
ADD, SUBTRACT, MULT = mybir.AluOpType.add, mybir.AluOpType.subtract, mybir.AluOpType.mult
SIGMOID, TANH = mybir.ActivationFunctionType.Sigmoid, mybir.ActivationFunctionType.Tanh
COPY = mybir.ActivationFunctionType.Copy

C = 128
S = 1024
N = 1024
CHUNK = 256
CHUNKS = N // CHUNK
PIECE = 512
PSUM_BANKS = 8
WARM_MATMULS = 16

FLOPS = 2 * C * C * N + 2 * 2 * C * 3 * C * N


def tile_denseggnn_kernel(tc, x, w, w_ih, w_hh, b_ih, b_hh, offs, out):
    nc = tc.nc
    with (
        tc.tile_pool(name="held", bufs=1) as held,
        tc.tile_pool(name="work", bufs=CHUNKS) as work,
        tc.psum_pool(name="banks", bufs=PSUM_BANKS) as banks,
    ):
        offsets = held.tile([C, N // 16], U16, name="offsets")
        nc.sync.dma_start(offsets[:], offs)
        x_sb = held.tile([C, S], BF16, name="x_sb")
        nc.scalar.dma_start(x_sb[:], x)
        w_sb = held.tile([C, C], BF16, name="w_sb")
        nc.sync.dma_start(w_sb[:], w)
        w_hh_sb = held.tile([C, 3 * C], BF16, name="w_hh_sb")
        nc.scalar.dma_start(w_hh_sb[:], w_hh)
        w_ih_sb = held.tile([C, 3 * C], BF16, name="w_ih_sb")
        nc.scalar.dma_start(w_ih_sb[:], w_ih)

        bias_ih = held.tile([C, 3], F32, name="bias_ih")
        bias_hh = held.tile([C, 3], F32, name="bias_hh")
        with nc.allow_non_contiguous_dma(reason="one bias value for each partition"):
            nc.sync.dma_start(bias_ih[:], b_ih.rearrange("(g c) o -> c (g o)", c=C))
            nc.sync.dma_start(bias_hh[:], b_hh.rearrange("(g c) o -> c (g o)", c=C))

        zeros = held.tile([C, C], BF16, name="zeros")
        nc.vector.memset(zeros[:], 0.0)
        idle_ps = banks.tile([C, C], F32, name="idle_ps", tag="bank")
        for i in range(WARM_MATMULS):
            nc.tensor.matmul(idle_ps[:], zeros[:], zeros[:], start=True, stop=True)
        idle_act = held.tile([C, 1], F32, name="idle_act")
        nc.scalar.activation(idle_act[:], zeros[:, 0:1], SIGMOID)

        ident = held.tile([C, C], F32, name="ident")
        make_identity(nc, ident[:])

        own = [x_sb[:, c * CHUNK : (c + 1) * CHUNK] for c in range(CHUNKS)]

        m_bf = [held.tile([C, CHUNK], BF16, name=f"m_bf{c}") for c in range(CHUNKS)]
        for p in range(N // PIECE):
            m_ps = banks.tile([C, PIECE], F32, name=f"m_ps{p}", tag="bank")
            picked = x_sb[:].indirect(offsets[:, p * (PIECE // 16) : (p + 1) * (PIECE // 16)])
            nc.tensor.matmul(m_ps[:], w_sb[:], picked, start=True, stop=True)
            for half in range(PIECE // CHUNK):
                c = p * (PIECE // CHUNK) + half
                if p % 2 == 0:
                    nc.vector.tensor_copy(m_bf[c][:], m_ps[:, half * CHUNK : (half + 1) * CHUNK])
                else:
                    nc.scalar.activation(m_bf[c][:], m_ps[:, half * CHUNK : (half + 1) * CHUNK], COPY)

        bias_rz = held.tile([C, 2], F32, name="bias_rz")
        nc.vector.tensor_tensor(bias_rz[:], bias_ih[:, 0:2], bias_hh[:, 0:2], ADD)

        w_r, w_z, w_n = slice(0, C), slice(C, 2 * C), slice(2 * C, 3 * C)
        gated, z, summed = {}, {}, {}

        for ahead in range(CHUNKS + 1):
            behind = ahead - 1
            if ahead < CHUNKS:
                c = ahead
                r_ps = banks.tile([C, CHUNK], F32, name=f"r_ps{c}", tag="bank")
                nc.tensor.matmul(r_ps[:], w_hh_sb[:, w_r], own[c], start=True, stop=False)
                nc.tensor.matmul(r_ps[:], w_ih_sb[:, w_r], m_bf[c][:], start=False, stop=True)
                vn_ps = banks.tile([C, CHUNK], F32, name=f"vn_ps{c}", tag="bank")
                nc.tensor.matmul(vn_ps[:], w_hh_sb[:, w_n], own[c], start=True, stop=True)
                r = work.tile([C, CHUNK], F32, name="r")
                nc.scalar.activation(r[:], r_ps[:], SIGMOID, bias=bias_rz[:, 0:1])
                gated[c] = work.tile([C, CHUNK], F32, name="gated")
                nc.vector.scalar_tensor_tensor(gated[c][:], vn_ps[:], bias_hh[:, 2:3], r[:], ADD, MULT)
            if behind >= 0:
                c = behind
                z_ps = banks.tile([C, CHUNK], F32, name=f"z_ps{c}", tag="bank")
                nc.tensor.matmul(z_ps[:], w_hh_sb[:, w_z], own[c], start=True, stop=False)
                nc.tensor.matmul(z_ps[:], w_ih_sb[:, w_z], m_bf[c][:], start=False, stop=True)
                z[c] = work.tile([C, CHUNK], F32, name="z")
                nc.scalar.activation(z[c][:], z_ps[:], SIGMOID, bias=bias_rz[:, 1:2])
                on_vector = c == 0
                un_ps = banks.tile([C, CHUNK], F32, name=f"un_ps{c}", tag="bank")
                nc.tensor.matmul(un_ps[:], w_ih_sb[:, w_n], m_bf[c][:], start=True, stop=on_vector)
                if on_vector:
                    summed[c] = work.tile([C, CHUNK], F32, name="pre")
                    nc.vector.tensor_tensor(summed[c][:], un_ps[:], gated[c][:], ADD)
                else:
                    nc.tensor.matmul(un_ps[:], ident[:], gated[c][:], start=False, stop=True)
                    summed[c] = un_ps

        for c in range(CHUNKS):
            cand = work.tile([C, CHUNK], F32, name="cand")
            nc.scalar.activation(cand[:], summed[c][:], TANH, bias=bias_ih[:, 2:3])
            kept = work.tile([C, CHUNK], F32, name="kept")
            nc.vector.tensor_tensor(kept[:], z[c][:], own[c], MULT)
            step = work.tile([C, CHUNK], F32, name="step")
            nc.vector.scalar_tensor_tensor(step[:], z[c][:], 1.0, cand[:], SUBTRACT, MULT)
            new = work.tile([C, CHUNK], F32, name="new")
            nc.vector.tensor_tensor(new[:], kept[:], step[:], SUBTRACT)
            nc.sync.dma_start(out[:, c * CHUNK : (c + 1) * CHUNK], new[:])
